import numpy as np
import ml_dtypes

BF16 = ml_dtypes.bfloat16


def bf(x):
    return np.asarray(x, np.float32).astype(BF16)


def f32(x):
    return np.asarray(x, np.float32)


def f64(x):
    return np.asarray(x).astype(np.float64)


def striped(idx):
    return np.tile(idx.reshape(-1, 16).T, (8, 1))


D, S, N, F, T, P = 128, 512, 128, 128, 4, 2


def setup_inputs():
    return {"table": bf(np.random.standard_normal((D, S))), "w": bf(np.random.uniform(-1.0, 1.0, (D, T * F)) / np.sqrt(T * D)), "b": f32(0.1 * np.random.standard_normal((F, 1))), "offs": striped(np.random.permutation(S)[:N])}


def reference(table, w, b, offs):
    idx = offs[:16].T.reshape(-1)
    y = f64(w).T @ f64(table)[:, idx]
    res = np.zeros((F, N)) + f64(b)
    for t in range(T):
        d = t - P
        lo, hi = max(0, -d), min(N, N - d)
        res[:, lo:hi] += y[t * F:(t + 1) * F, lo + d:hi + d]
    return res

@@ -1,0 +1,55 @@
+import concourse.mybir as mybir
+
+BF16, F32, U16 = mybir.dt.bfloat16, mybir.dt.float32, mybir.dt.uint16
+ADD = mybir.AluOpType.add
+
+FEATURES = 128
+WORDS = 512
+POSITIONS = 128
+FILTERS = 128
+TAPS = 4
+CENTRE = 2
+
+FLOPS = 2 * FEATURES * TAPS * FILTERS * POSITIONS
+
+
+def tile_qa_cnn_kernel(tc, table, w, b, offs, out):
+    nc = tc.nc
+    with (
+        tc.tile_pool(name="held", bufs=1) as held,
+        tc.psum_pool(name="psum", bufs=1) as psum,
+    ):
+        offsets = held.tile([FEATURES, POSITIONS // 16], U16, name="offsets")
+        nc.sync.dma_start(offsets[:], offs)
+        words = held.tile([FEATURES, WORDS], BF16, name="words")
+        nc.sync.dma_start(words[:], table)
+        weights = held.tile([FEATURES, TAPS * FILTERS], BF16, name="weights")
+        nc.scalar.dma_start(weights[:], w)
+        bias = held.tile([FILTERS, 1], F32, name="bias")
+        nc.scalar.dma_start(bias[:], b)
+
+        order = [CENTRE] + [t for t in range(TAPS) if t != CENTRE]
+
+        products = {}
+        for t in order:
+            products[t] = psum.tile([FILTERS, POSITIONS], F32, name=f"product{t}")
+            nc.tensor.matmul(
+                products[t][:],
+                weights[:, t * FILTERS : (t + 1) * FILTERS],
+                words[:].indirect(offsets[:]),
+                start=True,
+                stop=True,
+            )
+
+        result = held.tile([FILTERS, POSITIONS], F32, name="result")
+        nc.vector.tensor_scalar(result[:], products[CENTRE][:], bias[:, 0:1], None, ADD)
+        for t in order[1:]:
+            shift = t - CENTRE
+            first, last = max(0, -shift), min(POSITIONS, POSITIONS - shift)
+            nc.vector.tensor_tensor(
+                result[:, first:last],
+                products[t][:, first + shift : last + shift],
+                result[:, first:last],
+                ADD,
+            )
+        nc.sync.dma_start(out, result[:])

@@ -9,6 +9,9 @@ POSITIONS = 128
 FILTERS = 128
 TAPS = 4
 CENTRE = 2
+PIECE = 64
+MARGIN = TAPS - 1 - CENTRE
+PADDED = POSITIONS + TAPS
 
 FLOPS = 2 * FEATURES * TAPS * FILTERS * POSITIONS
 
@@ -28,28 +31,24 @@ def tile_qa_cnn_kernel(tc, table, w, b, offs, out):
         bias = held.tile([FILTERS, 1], F32, name="bias")
         nc.scalar.dma_start(bias[:], b)
 
-        order = [CENTRE] + [t for t in range(TAPS) if t != CENTRE]
+        zeros = held.tile([FEATURES, PADDED], BF16, name="zeros")
+        nc.vector.memset(zeros[:], 0.0)
+        total = psum.tile([FILTERS, PADDED], F32, name="total")
+        nc.tensor.matmul(total[:], zeros[:, 0:FILTERS], zeros[:], start=True, stop=False)
 
-        products = {}
-        for t in order:
-            products[t] = psum.tile([FILTERS, POSITIONS], F32, name=f"product{t}")
+        pieces = [(t, i) for t in range(TAPS) for i in range(0, POSITIONS, PIECE)]
+        for t, i in pieces:
+            column = i + CENTRE - t + MARGIN
             nc.tensor.matmul(
-                products[t][:],
+                total[:, column : column + PIECE],
                 weights[:, t * FILTERS : (t + 1) * FILTERS],
-                words[:].indirect(offsets[:]),
-                start=True,
-                stop=True,
+                words[:].indirect(offsets[:, i // 16 : (i + PIECE) // 16]),
+                start=False,
+                stop=(t, i) == pieces[-1],
             )
 
         result = held.tile([FILTERS, POSITIONS], F32, name="result")
-        nc.vector.tensor_scalar(result[:], products[CENTRE][:], bias[:, 0:1], None, ADD)
-        for t in order[1:]:
-            shift = t - CENTRE
-            first, last = max(0, -shift), min(POSITIONS, POSITIONS - shift)
-            nc.vector.tensor_tensor(
-                result[:, first:last],
-                products[t][:, first + shift : last + shift],
-                result[:, first:last],
-                ADD,
-            )
+        nc.vector.tensor_scalar(
+            result[:], total[:, MARGIN : MARGIN + POSITIONS], bias[:, 0:1], None, ADD
+        )
         nc.sync.dma_start(out, result[:])

@@ -27,7 +27,8 @@ def tile_qa_cnn_kernel(tc, table, w, b, offs, out):
         words = held.tile([FEATURES, WORDS], BF16, name="words")
         nc.sync.dma_start(words[:], table)
         weights = held.tile([FEATURES, TAPS * FILTERS], BF16, name="weights")
-        nc.scalar.dma_start(weights[:], w)
+        nc.scalar.dma_start(weights[:, 0:FILTERS], w[:, 0:FILTERS])
+        nc.sync.dma_start(weights[:, FILTERS:], w[:, FILTERS:])
         bias = held.tile([FILTERS, 1], F32, name="bias")
         nc.scalar.dma_start(bias[:], b)
 

@@ -27,10 +27,10 @@ def tile_qa_cnn_kernel(tc, table, w, b, offs, out):
         words = held.tile([FEATURES, WORDS], BF16, name="words")
         nc.sync.dma_start(words[:], table)
         weights = held.tile([FEATURES, TAPS * FILTERS], BF16, name="weights")
-        nc.scalar.dma_start(weights[:, 0:FILTERS], w[:, 0:FILTERS])
+        nc.sync.dma_start(weights[:, 0:FILTERS], w[:, 0:FILTERS])
         nc.sync.dma_start(weights[:, FILTERS:], w[:, FILTERS:])
         bias = held.tile([FILTERS, 1], F32, name="bias")
-        nc.scalar.dma_start(bias[:], b)
+        nc.sync.dma_start(bias[:], b)
 
         zeros = held.tile([FEATURES, PADDED], BF16, name="zeros")
         nc.vector.memset(zeros[:], 0.0)

import concourse.mybir as mybir

BF16, F32, U16 = mybir.dt.bfloat16, mybir.dt.float32, mybir.dt.uint16
ADD = mybir.AluOpType.add

FEATURES = 128
WORDS = 512
POSITIONS = 128
FILTERS = 128
TAPS = 4
CENTRE = 2
PIECE = 64
MARGIN = TAPS - 1 - CENTRE
PADDED = POSITIONS + TAPS

FLOPS = 2 * FEATURES * TAPS * FILTERS * POSITIONS


def tile_qa_cnn_kernel(tc, table, w, b, offs, out):
    nc = tc.nc
    with (
        tc.tile_pool(name="held", bufs=1) as held,
        tc.psum_pool(name="psum", bufs=1) as psum,
    ):
        offsets = held.tile([FEATURES, POSITIONS // 16], U16, name="offsets")
        nc.sync.dma_start(offsets[:], offs)
        words = held.tile([FEATURES, WORDS], BF16, name="words")
        nc.sync.dma_start(words[:], table)
        weights = held.tile([FEATURES, TAPS * FILTERS], BF16, name="weights")
        nc.sync.dma_start(weights[:, 0:FILTERS], w[:, 0:FILTERS])
        nc.sync.dma_start(weights[:, FILTERS:], w[:, FILTERS:])
        bias = held.tile([FILTERS, 1], F32, name="bias")
        nc.sync.dma_start(bias[:], b)

        zeros = held.tile([FEATURES, PADDED], BF16, name="zeros")
        nc.vector.memset(zeros[:], 0.0)
        total = psum.tile([FILTERS, PADDED], F32, name="total")
        nc.tensor.matmul(total[:], zeros[:, 0:FILTERS], zeros[:], start=True, stop=False)

        pieces = [(t, i) for t in range(TAPS) for i in range(0, POSITIONS, PIECE)]
        for t, i in pieces:
            column = i + CENTRE - t + MARGIN
            nc.tensor.matmul(
                total[:, column : column + PIECE],
                weights[:, t * FILTERS : (t + 1) * FILTERS],
                words[:].indirect(offsets[:, i // 16 : (i + PIECE) // 16]),
                start=False,
                stop=(t, i) == pieces[-1],
            )

        result = held.tile([FILTERS, POSITIONS], F32, name="result")
        nc.vector.tensor_scalar(
            result[:], total[:, MARGIN : MARGIN + POSITIONS], bias[:, 0:1], None, ADD
        )
        nc.sync.dma_start(out, result[:])
